import numpy as np
import ml_dtypes


def mxq(x, axis, fmt="e4m3"):
    dtype, down = {"e4m3": (ml_dtypes.float8_e4m3fn, 7), "e5m2": (ml_dtypes.float8_e5m2, 14)}[fmt]
    v = np.moveaxis(np.asarray(x, np.float32).astype(ml_dtypes.bfloat16).astype(np.float64), axis, -1)
    blocks = v.reshape(v.shape[:-1] + (-1, 32))
    amax = np.abs(blocks).max(-1, keepdims=True)
    byte = np.maximum(np.where(amax > 0, np.frexp(amax)[1] - 1 + 127, 0) - down, 1)
    scale = np.exp2(byte - 127.0)
    codes = (blocks / scale).astype(np.float32).astype(dtype).astype(np.float64)
    return np.moveaxis((codes * scale).reshape(v.shape), -1, axis)


WIDE = False


def mx_kscale(k):
    if not WIDE:
        return np.ones(k)
    levels = np.array([10, -10, 5, -5, 0])
    a = np.random.permutation(np.resize(levels, k // 512 * 4)).reshape(k // 512, 4)
    idx = np.arange(k)
    return np.exp2(a[idx // 512, idx % 128 // 32])


BF16 = ml_dtypes.bfloat16


def bf(x):
    return np.asarray(x, np.float32).astype(BF16)


def f64(x):
    return np.asarray(x).astype(np.float64)


E2M1 = np.array([0.0, 0.5, 1.0, 1.5, 2.0, 3.0, 4.0, 6.0, -0.0, -0.5, -1.0, -1.5, -2.0, -3.0, -4.0, -6.0])


def pack_weight(w, fmt):
    k, n = w.shape
    w = f64(bf(w)).reshape(k // 32, 32, n)
    amax = np.abs(w).max(1)
    if fmt == "e4m3":
        byte = np.frexp(amax)[1] - 1 + 127 - 7
    else:
        mant, ex = np.frexp(amax / 6.0)
        byte = np.where(mant > 0.5, ex, ex - 1) + 127
    byte = np.clip(np.where(amax > 0, byte, 1), 1, 254)
    scaled = (w * np.exp2(127.0 - byte)[:, None, :]).reshape(k, n).astype(np.float32)
    by_word = np.ascontiguousarray(scaled.reshape(k // 512, 128, 4, n).transpose(0, 1, 3, 2))
    if fmt == "e4m3":
        words = by_word.astype(ml_dtypes.float8_e4m3fn).view(np.uint8)
    else:
        c = by_word.astype(ml_dtypes.float4_e2m1fn).view(np.uint8) & 0xF
        words = c[..., 0::2] | (c[..., 1::2] << 4)
    return np.ascontiguousarray(words), np.ascontiguousarray(byte.astype(np.uint8).reshape(k // 512, 16, n))


def unpack_weight(words, scales, fmt):
    g, p, n, _ = words.shape
    if fmt == "e4m3":
        vals = np.ascontiguousarray(words).view(ml_dtypes.float8_e4m3fn).astype(np.float64)
    else:
        nib = np.empty((g, p, n, 4), np.uint8)
        nib[..., 0::2] = words & 0xF
        nib[..., 1::2] = words >> 4
        vals = E2M1[nib]
    vals = vals * np.repeat(np.exp2(scales.astype(np.float64) - 127.0), 8, axis=1)[..., None]
    return vals.transpose(0, 1, 3, 2).reshape(g * 512, n)


B, L, D, H, HD, FF = 4, 1024, 1024, 2, 128, 4096
EPS = 1e-6
DA = H * HD


def rmsnorm(x, w):
    return x * (1.0 / np.sqrt(np.mean(x * x, axis=-1, keepdims=True) + EPS)) * w


def setup_inputs():
    s = mx_kscale(D)
    x = bf(np.random.standard_normal((B, L, D)))
    norm1_w = bf((1.0 + 0.1 * np.random.standard_normal(D)) * s)
    qkv_w = np.random.standard_normal((3 * DA, D)) / np.sqrt(D) / s[None, :]
    words, scales = pack_weight(np.ascontiguousarray(qkv_w.T), "e4m3")
    return {"x": x,
            "norm1_w": norm1_w,
            "qkv_w_words": words,
            "qkv_w_scales": scales}


def reference(x, norm1_w, qkv_w_words, qkv_w_scales):
    h = rmsnorm(f64(x), f64(norm1_w))
    qkv = mxq(h, 2, "e4m3") @ unpack_weight(qkv_w_words, qkv_w_scales, "e4m3")
    qkv = qkv.reshape(B, L, 3, H, HD)
    q, k, v = (np.moveaxis(qkv, 2, 0)[i].transpose(0, 2, 1, 3) for i in range(3))
    return q, k, v

@@ -1,0 +1,206 @@
+from contextlib import ExitStack
+
+import concourse.mybir as mybir
+from concourse.masks import make_identity
+
+BF16 = mybir.dt.bfloat16
+F32 = mybir.dt.float32
+I32 = mybir.dt.int32
+U32 = mybir.dt.uint32
+U8 = mybir.dt.uint8
+FP8X4 = mybir.dt.float8_e4m3fn_x4
+ACT = mybir.ActivationFunctionType
+MULT = mybir.AluOpType.mult
+
+P = 128
+BATCH = 4
+SEQ = 1024
+DIM = 1024
+HEADS = 2
+HEAD_DIM = 128
+EPS = 1e-6
+FEATURES = 3 * HEADS * HEAD_DIM
+BLOCKS = FEATURES // HEAD_DIM
+K_PASS = 4 * P
+PASSES = DIM // K_PASS
+WORDS = K_PASS // 2
+TILES_PER_BATCH = SEQ // P
+TILES = BATCH * TILES_PER_BATCH
+PAIR = 2
+WIDE = 512
+
+FLOPS = 2 * BATCH * SEQ * DIM * FEATURES
+
+SQUARES_AHEAD = 4
+INVERT_AHEAD = 3
+REGROUP_BEHIND = 1
+QUANTISE_BEHIND = 2
+DRAIN_BEHIND = 3
+
+
+def tile_transformerblock_pa_t_kernel(
+    tc, x, norm1_w, qkv_w_words, qkv_w_scales, out_0, out_1, out_2
+):
+    nc = tc.nc
+    x_rows = x.rearrange("b (p t) d -> b p t d", t=TILES_PER_BATCH)
+    out_rows = [
+        o.rearrange("b n (p t) j -> b p n t j", t=TILES_PER_BATCH) for o in (out_0, out_1, out_2)
+    ]
+
+    with ExitStack() as ctx:
+        ctx.enter_context(tc.manual_schedule())
+        keep = ctx.enter_context(tc.tile_pool(name="keep", bufs=1))
+        ring = ctx.enter_context(tc.tile_pool(name="ring", bufs=3))
+        results = ctx.enter_context(tc.tile_pool(name="results", bufs=4))
+        flipped = ctx.enter_context(tc.psum_pool(name="flipped", bufs=2))
+        products = ctx.enter_context(tc.psum_pool(name="products", bufs=2))
+
+        x_all = keep.tile([P, TILES, DIM], BF16)
+        gain = keep.tile([P, DIM], BF16)
+        w_words = keep.tile([P, PASSES, FEATURES], U32, align_bytes=64)
+        w_scales = keep.tile([P, PASSES, FEATURES], U8, align_bytes=64)
+        identity = keep.tile([P, P], F32)
+        eps = keep.tile([P, 1], F32)
+        sumsq = keep.tile([P, TILES], F32)
+        rms = keep.tile([P, TILES], F32)
+        rstd = keep.tile([P, TILES], F32)
+
+        def load_pair(first):
+            b, t = divmod(first, TILES_PER_BATCH)
+            nc.sync.dma_start(
+                out=x_all[:, first : first + PAIR, :], in_=x_rows[b, :, t : t + PAIR, :]
+            )
+
+        nc.vector.memset(w_scales[:].bitcast(I32), 0)
+        nc.vector.memset(eps[:], EPS)
+        make_identity(nc, identity[:])
+
+        load_pair(0)
+        nc.scalar.dma_start(out=gain[:], in_=norm1_w.partition_broadcast(P))
+        load_pair(PAIR)
+        nc.sync.dma_start(
+            out=w_words[:].bitcast(I32),
+            in_=qkv_w_words.rearrange("g p n t -> p g (n t)").bitcast(I32),
+        )
+        for quadrant in range(4):
+            nc.sync.dma_start(
+                out=w_scales[32 * quadrant : 32 * quadrant + 4, :, :].bitcast(I32),
+                in_=qkv_w_scales[:, 4 * quadrant : 4 * quadrant + 4, :]
+                .rearrange("g r n -> r g n")
+                .bitcast(I32),
+            )
+        for first in range(2 * PAIR, TILES, PAIR):
+            load_pair(first)
+
+        h_of, flipped_of, grouped_of, codes_of, planes_of, product_of, result_of = (
+            {}, {}, {}, {}, {}, {}, {},
+        )
+
+        def square_sum(i):
+            squares = ring.tile([P, DIM], BF16)
+            nc.scalar.activation(
+                out=squares[:], in_=x_all[:, i, :], func=ACT.Square, accum_out=sumsq[:, i : i + 1]
+            )
+            if i % PAIR == PAIR - 1:
+                pair = slice(i + 1 - PAIR, i + 1)
+                nc.scalar.activation(
+                    out=rms[:, pair], in_=sumsq[:, pair], func=ACT.Sqrt,
+                    scale=1.0 / DIM, bias=eps[:, 0:1],
+                )
+
+        def invert(i):
+            if i % PAIR == PAIR - 1:
+                pair = slice(i + 1 - PAIR, i + 1)
+                nc.vector.reciprocal(out=rstd[:, pair], in_=rms[:, pair])
+
+        def scale(i):
+            h = ring.tile([P, DIM], BF16)
+            nc.vector.scalar_tensor_tensor(
+                out=h[:], in0=x_all[:, i, :], scalar=rstd[:, i : i + 1], in1=gain[:],
+                op0=MULT, op1=MULT,
+            )
+            h_of[i] = h
+
+        def flip(i):
+            words = h_of[i][:].bitcast(F32)
+            bank = flipped.tile([P, PASSES, 2, P], F32)
+            for g in range(PASSES):
+                for u in range(2):
+                    nc.tensor.transpose(
+                        out=bank[:, g, u, :],
+                        in_=words[:, WORDS * g + u : WORDS * (g + 1) : 2],
+                        identity=identity[:],
+                    )
+            flipped_of[i] = bank
+
+        def regroup(i):
+            grouped = ring.tile([P, PASSES, P, 4], BF16, align_bytes=64)
+            nc.vector.tensor_copy(
+                out=grouped[:].bitcast(F32),
+                in_=flipped_of[i][:].rearrange("p g u r -> p g r u"),
+            )
+            grouped_of[i] = grouped
+
+        def quantise(i):
+            codes = ring.tile([P, PASSES, P], U32, align_bytes=64)
+            planes = ring.tile([P, PASSES, P], U8, align_bytes=64)
+            nc.vector.quantize_mx(
+                out=codes[:].rearrange("p g r -> p (g r)").bitcast(FP8X4),
+                scales=planes[:].rearrange("p g r -> p (g r)"),
+                in_=grouped_of[i][:].rearrange("p g r t -> p (g r t)"),
+            )
+            codes_of[i], planes_of[i] = codes, planes
+
+        def project(i):
+            qk = products.tile([P, WIDE], F32)
+            v = products.tile([P, FEATURES - WIDE], F32)
+            for acc, cols in ((qk, slice(0, WIDE)), (v, slice(WIDE, FEATURES))):
+                for g in range(PASSES):
+                    nc.tensor.matmul_mx(
+                        out=acc[:],
+                        lhsT=codes_of[i][:, g, :].bitcast(FP8X4),
+                        lhsT_scale=planes_of[i][:, g, :],
+                        rhs=w_words[:, g, cols].bitcast(FP8X4),
+                        rhs_scale=w_scales[:, g, cols],
+                        start=(g == 0),
+                        stop=(g == PASSES - 1),
+                    )
+            product_of[i] = (qk, v)
+
+        def drain(i):
+            first = i - i % PAIR
+            if i == first:
+                result = results.tile([P, BLOCKS, PAIR, HEAD_DIM], F32)
+                result_of[first] = result
+            result = result_of[first]
+            qk, v = product_of[i]
+            split = WIDE // HEAD_DIM
+            nc.scalar.copy(
+                out=result[:, 0:split, i - first, :],
+                in_=qk[:].rearrange("p (c j) -> p c j", j=HEAD_DIM),
+            )
+            nc.scalar.copy(
+                out=result[:, split:BLOCKS, i - first, :],
+                in_=v[:].rearrange("p (c j) -> p c j", j=HEAD_DIM),
+            )
+            if i == first + PAIR - 1:
+                b, t = divmod(first, TILES_PER_BATCH)
+                for which in range(3):
+                    nc.sync.dma_start(
+                        out=out_rows[which][b, :, :, t : t + PAIR, :],
+                        in_=result[:, HEADS * which : HEADS * (which + 1), :, :],
+                    )
+
+        def run(stage, i):
+            if 0 <= i < TILES:
+                stage(i)
+
+        for step in range(-SQUARES_AHEAD, TILES + DRAIN_BEHIND):
+            run(square_sum, step + SQUARES_AHEAD)
+            run(scale, step)
+            run(flip, step)
+            run(regroup, step - REGROUP_BEHIND)
+            run(quantise, step - QUANTISE_BEHIND)
+            run(project, step - QUANTISE_BEHIND)
+            run(invert, step + INVERT_AHEAD)
+            run(drain, step - DRAIN_BEHIND)

@@ -32,7 +32,7 @@ WIDE = 512
 FLOPS = 2 * BATCH * SEQ * DIM * FEATURES
 
 SQUARES_AHEAD = 4
-INVERT_AHEAD = 3
+INVERT_AHEAD = 2
 REGROUP_BEHIND = 1
 QUANTISE_BEHIND = 2
 DRAIN_BEHIND = 3
@@ -53,31 +53,35 @@ def tile_transformerblock_pa_t_kernel(
         ring = ctx.enter_context(tc.tile_pool(name="ring", bufs=3))
         results = ctx.enter_context(tc.tile_pool(name="results", bufs=4))
         flipped = ctx.enter_context(tc.psum_pool(name="flipped", bufs=2))
-        products = ctx.enter_context(tc.psum_pool(name="products", bufs=2))
+        products = ctx.enter_context(tc.psum_pool(name="products", bufs=3))
 
         x_all = keep.tile([P, TILES, DIM], BF16)
+        gain_row = keep.tile([P, DIM], BF16)
+        ones = keep.tile([P, P], BF16)
         gain = keep.tile([P, DIM], BF16)
         w_words = keep.tile([P, PASSES, FEATURES], U32, align_bytes=64)
         w_scales = keep.tile([P, PASSES, FEATURES], U8, align_bytes=64)
         identity = keep.tile([P, P], F32)
         eps = keep.tile([P, 1], F32)
+        first_root = keep.tile([P, 1], F32)
         sumsq = keep.tile([P, TILES], F32)
         rms = keep.tile([P, TILES], F32)
         rstd = keep.tile([P, TILES], F32)
 
-        def load_pair(first):
-            b, t = divmod(first, TILES_PER_BATCH)
-            nc.sync.dma_start(
-                out=x_all[:, first : first + PAIR, :], in_=x_rows[b, :, t : t + PAIR, :]
-            )
+        def load(i):
+            b, t = divmod(i, TILES_PER_BATCH)
+            nc.sync.dma_start(out=x_all[:, i, :], in_=x_rows[b, :, t, :])
 
-        nc.vector.memset(w_scales[:].bitcast(I32), 0)
         nc.vector.memset(eps[:], EPS)
+        nc.vector.memset(gain_row[:], 0.0)
+        nc.vector.memset(ones[:], 1.0)
+        nc.vector.memset(w_scales[:].bitcast(I32), 0)
         make_identity(nc, identity[:])
+        nc.scalar.activation(out=first_root[:], in_=eps[:], func=ACT.Sqrt)
 
-        load_pair(0)
-        nc.scalar.dma_start(out=gain[:], in_=norm1_w.partition_broadcast(P))
-        load_pair(PAIR)
+        load(0)
+        nc.sync.dma_start(out=gain_row[0:1, :], in_=norm1_w.rearrange("(o d) -> o d", o=1))
+        load(1)
         nc.sync.dma_start(
             out=w_words[:].bitcast(I32),
             in_=qkv_w_words.rearrange("g p n t -> p g (n t)").bitcast(I32),
@@ -89,8 +93,13 @@ def tile_transformerblock_pa_t_kernel(
                 .rearrange("g r n -> r g n")
                 .bitcast(I32),
             )
-        for first in range(2 * PAIR, TILES, PAIR):
-            load_pair(first)
+        for i in range(2, TILES):
+            load(i)
+
+        for cols in (slice(0, WIDE), slice(WIDE, DIM)):
+            spread = products.tile([P, WIDE], F32, tag="qk")
+            nc.tensor.matmul(out=spread[:], lhsT=ones[:], rhs=gain_row[:, cols], start=True, stop=True)
+            nc.vector.tensor_copy(out=gain[:, cols], in_=spread[:])
 
         h_of, flipped_of, grouped_of, codes_of, planes_of, product_of, result_of = (
             {}, {}, {}, {}, {}, {}, {},
@@ -101,6 +110,8 @@ def tile_transformerblock_pa_t_kernel(
             nc.scalar.activation(
                 out=squares[:], in_=x_all[:, i, :], func=ACT.Square, accum_out=sumsq[:, i : i + 1]
             )
+
+        def root(i):
             if i % PAIR == PAIR - 1:
                 pair = slice(i + 1 - PAIR, i + 1)
                 nc.scalar.activation(
@@ -135,7 +146,8 @@ def tile_transformerblock_pa_t_kernel(
 
         def regroup(i):
             grouped = ring.tile([P, PASSES, P, 4], BF16, align_bytes=64)
-            nc.vector.tensor_copy(
+            copy = nc.vector.tensor_copy if i < TILES - SQUARES_AHEAD else nc.scalar.copy
+            copy(
                 out=grouped[:].bitcast(F32),
                 in_=flipped_of[i][:].rearrange("p g u r -> p g r u"),
             )
@@ -199,8 +211,9 @@ def tile_transformerblock_pa_t_kernel(
             run(square_sum, step + SQUARES_AHEAD)
             run(scale, step)
             run(flip, step)
-            run(regroup, step - REGROUP_BEHIND)
             run(quantise, step - QUANTISE_BEHIND)
             run(project, step - QUANTISE_BEHIND)
+            run(regroup, step - REGROUP_BEHIND)
             run(invert, step + INVERT_AHEAD)
             run(drain, step - DRAIN_BEHIND)
+            run(root, step + SQUARES_AHEAD)

@@ -211,9 +211,9 @@ def tile_transformerblock_pa_t_kernel(
             run(square_sum, step + SQUARES_AHEAD)
             run(scale, step)
             run(flip, step)
+            run(invert, step + INVERT_AHEAD)
             run(quantise, step - QUANTISE_BEHIND)
             run(project, step - QUANTISE_BEHIND)
             run(regroup, step - REGROUP_BEHIND)
-            run(invert, step + INVERT_AHEAD)
             run(drain, step - DRAIN_BEHIND)
             run(root, step + SQUARES_AHEAD)

@@ -81,7 +81,8 @@ def tile_transformerblock_pa_t_kernel(
 
         load(0)
         nc.sync.dma_start(out=gain_row[0:1, :], in_=norm1_w.rearrange("(o d) -> o d", o=1))
-        load(1)
+        for i in range(1, SQUARES_AHEAD):
+            load(i)
         nc.sync.dma_start(
             out=w_words[:].bitcast(I32),
             in_=qkv_w_words.rearrange("g p n t -> p g (n t)").bitcast(I32),
@@ -93,7 +94,7 @@ def tile_transformerblock_pa_t_kernel(
                 .rearrange("g r n -> r g n")
                 .bitcast(I32),
             )
-        for i in range(2, TILES):
+        for i in range(SQUARES_AHEAD, TILES):
             load(i)
 
         for cols in (slice(0, WIDE), slice(WIDE, DIM)):

@@ -21,9 +21,9 @@ HEAD_DIM = 128
 EPS = 1e-6
 FEATURES = 3 * HEADS * HEAD_DIM
 BLOCKS = FEATURES // HEAD_DIM
-K_PASS = 4 * P
+PACK = 4
+K_PASS = PACK * P
 PASSES = DIM // K_PASS
-WORDS = K_PASS // 2
 TILES_PER_BATCH = SEQ // P
 TILES = BATCH * TILES_PER_BATCH
 PAIR = 2
@@ -31,8 +31,9 @@ WIDE = 512
 
 FLOPS = 2 * BATCH * SEQ * DIM * FEATURES
 
-SQUARES_AHEAD = 4
-INVERT_AHEAD = 2
+SQUARES_AHEAD = 5
+INVERT_AHEAD = 3
+SCALE_AHEAD = 1
 REGROUP_BEHIND = 1
 QUANTISE_BEHIND = 2
 DRAIN_BEHIND = 3
@@ -52,13 +53,11 @@ def tile_transformerblock_pa_t_kernel(
         keep = ctx.enter_context(tc.tile_pool(name="keep", bufs=1))
         ring = ctx.enter_context(tc.tile_pool(name="ring", bufs=3))
         results = ctx.enter_context(tc.tile_pool(name="results", bufs=4))
-        flipped = ctx.enter_context(tc.psum_pool(name="flipped", bufs=2))
-        products = ctx.enter_context(tc.psum_pool(name="products", bufs=3))
+        flipped = ctx.enter_context(tc.psum_pool(name="flipped", bufs=2 * PASSES))
+        products = ctx.enter_context(tc.psum_pool(name="products", bufs=2))
 
         x_all = keep.tile([P, TILES, DIM], BF16)
-        gain_row = keep.tile([P, DIM], BF16)
-        ones = keep.tile([P, P], BF16)
-        gain = keep.tile([P, DIM], BF16)
+        gain = keep.tile([P, PASSES, PACK], BF16)
         w_words = keep.tile([P, PASSES, FEATURES], U32, align_bytes=64)
         w_scales = keep.tile([P, PASSES, FEATURES], U8, align_bytes=64)
         identity = keep.tile([P, P], F32)
@@ -73,16 +72,16 @@ def tile_transformerblock_pa_t_kernel(
             nc.sync.dma_start(out=x_all[:, i, :], in_=x_rows[b, :, t, :])
 
         nc.vector.memset(eps[:], EPS)
-        nc.vector.memset(gain_row[:], 0.0)
-        nc.vector.memset(ones[:], 1.0)
         nc.vector.memset(w_scales[:].bitcast(I32), 0)
         make_identity(nc, identity[:])
         nc.scalar.activation(out=first_root[:], in_=eps[:], func=ACT.Sqrt)
 
-        load(0)
-        nc.sync.dma_start(out=gain_row[0:1, :], in_=norm1_w.rearrange("(o d) -> o d", o=1))
-        for i in range(1, SQUARES_AHEAD):
+        for i in range(SQUARES_AHEAD):
             load(i)
+        with nc.allow_non_contiguous_dma(reason="the gain: 256 runs of four values, once"):
+            nc.sync.dma_start(
+                out=gain[:], in_=norm1_w.rearrange("(g p j) -> p g j", g=PASSES, j=PACK)
+            )
         nc.sync.dma_start(
             out=w_words[:].bitcast(I32),
             in_=qkv_w_words.rearrange("g p n t -> p g (n t)").bitcast(I32),
@@ -97,12 +96,7 @@ def tile_transformerblock_pa_t_kernel(
         for i in range(SQUARES_AHEAD, TILES):
             load(i)
 
-        for cols in (slice(0, WIDE), slice(WIDE, DIM)):
-            spread = products.tile([P, WIDE], F32, tag="qk")
-            nc.tensor.matmul(out=spread[:], lhsT=ones[:], rhs=gain_row[:, cols], start=True, stop=True)
-            nc.vector.tensor_copy(out=gain[:, cols], in_=spread[:])
-
-        h_of, flipped_of, grouped_of, codes_of, planes_of, product_of, result_of = (
+        y_of, flipped_of, grouped_of, codes_of, planes_of, product_of, result_of = (
             {}, {}, {}, {}, {}, {}, {},
         )
 
@@ -126,32 +120,34 @@ def tile_transformerblock_pa_t_kernel(
                 nc.vector.reciprocal(out=rstd[:, pair], in_=rms[:, pair])
 
         def scale(i):
-            h = ring.tile([P, DIM], BF16)
-            nc.vector.scalar_tensor_tensor(
-                out=h[:], in0=x_all[:, i, :], scalar=rstd[:, i : i + 1], in1=gain[:],
-                op0=MULT, op1=MULT,
+            y = ring.tile([P, PASSES, PACK, P], F32)
+            nc.gpsimd.tensor_scalar(
+                out=y[:],
+                in0=x_all[:, i, :].rearrange("p (g q j) -> p g j q", g=PASSES, j=PACK),
+                scalar1=rstd[:, i : i + 1], scalar2=1.0, op0=MULT, op1=MULT,
             )
-            h_of[i] = h
+            y_of[i] = y
 
         def flip(i):
-            words = h_of[i][:].bitcast(F32)
-            bank = flipped.tile([P, PASSES, 2, P], F32)
+            banks = []
             for g in range(PASSES):
-                for u in range(2):
+                bank = flipped.tile([P, PACK, P], F32)
+                for j in range(PACK):
                     nc.tensor.transpose(
-                        out=bank[:, g, u, :],
-                        in_=words[:, WORDS * g + u : WORDS * (g + 1) : 2],
-                        identity=identity[:],
+                        out=bank[:, j, :], in_=y_of[i][:, g, j, :], identity=identity[:]
                     )
-            flipped_of[i] = bank
+                banks.append(bank)
+            flipped_of[i] = banks
 
         def regroup(i):
-            grouped = ring.tile([P, PASSES, P, 4], BF16, align_bytes=64)
-            copy = nc.vector.tensor_copy if i < TILES - SQUARES_AHEAD else nc.scalar.copy
-            copy(
-                out=grouped[:].bitcast(F32),
-                in_=flipped_of[i][:].rearrange("p g u r -> p g r u"),
-            )
+            grouped = ring.tile([P, PASSES, P, PACK], BF16, align_bytes=64)
+            for g in range(PASSES):
+                nc.vector.tensor_tensor(
+                    out=grouped[:, g, :, :],
+                    in0=flipped_of[i][g][:].rearrange("p j r -> p r j"),
+                    in1=gain[:, g, :].unsqueeze(1).to_broadcast([P, P, PACK]),
+                    op=MULT,
+                )
             grouped_of[i] = grouped
 
         def quantise(i):
@@ -160,7 +156,7 @@ def tile_transformerblock_pa_t_kernel(
             nc.vector.quantize_mx(
                 out=codes[:].rearrange("p g r -> p (g r)").bitcast(FP8X4),
                 scales=planes[:].rearrange("p g r -> p (g r)"),
-                in_=grouped_of[i][:].rearrange("p g r t -> p (g r t)"),
+                in_=grouped_of[i][:].rearrange("p g r j -> p (g r j)"),
             )
             codes_of[i], planes_of[i] = codes, planes
 
@@ -186,23 +182,19 @@ def tile_transformerblock_pa_t_kernel(
                 result = results.tile([P, BLOCKS, PAIR, HEAD_DIM], F32)
                 result_of[first] = result
             result = result_of[first]
+            b, t = divmod(first, TILES_PER_BATCH)
             qk, v = product_of[i]
-            split = WIDE // HEAD_DIM
-            nc.scalar.copy(
-                out=result[:, 0:split, i - first, :],
-                in_=qk[:].rearrange("p (c j) -> p c j", j=HEAD_DIM),
-            )
-            nc.scalar.copy(
-                out=result[:, split:BLOCKS, i - first, :],
-                in_=v[:].rearrange("p (c j) -> p c j", j=HEAD_DIM),
-            )
-            if i == first + PAIR - 1:
-                b, t = divmod(first, TILES_PER_BATCH)
-                for which in range(3):
-                    nc.sync.dma_start(
-                        out=out_rows[which][b, :, :, t : t + PAIR, :],
-                        in_=result[:, HEADS * which : HEADS * (which + 1), :, :],
-                    )
+            for copy, bank, lo, hi in ((nc.scalar.copy, qk, 0, 2), (nc.vector.tensor_copy, v, 2, 3)):
+                copy(
+                    out=result[:, HEADS * lo : HEADS * hi, i - first, :],
+                    in_=bank[:].rearrange("p (c j) -> p c j", j=HEAD_DIM),
+                )
+                if i == first + PAIR - 1:
+                    for which in range(lo, hi):
+                        nc.sync.dma_start(
+                            out=out_rows[which][b, :, :, t : t + PAIR, :],
+                            in_=result[:, HEADS * which : HEADS * (which + 1), :, :],
+                        )
 
         def run(stage, i):
             if 0 <= i < TILES:
@@ -210,11 +202,11 @@ def tile_transformerblock_pa_t_kernel(
 
         for step in range(-SQUARES_AHEAD, TILES + DRAIN_BEHIND):
             run(square_sum, step + SQUARES_AHEAD)
-            run(scale, step)
+            run(scale, step + SCALE_AHEAD)
             run(flip, step)
-            run(invert, step + INVERT_AHEAD)
             run(quantise, step - QUANTISE_BEHIND)
             run(project, step - QUANTISE_BEHIND)
             run(regroup, step - REGROUP_BEHIND)
             run(drain, step - DRAIN_BEHIND)
+            run(invert, step + INVERT_AHEAD)
             run(root, step + SQUARES_AHEAD)

@@ -31,7 +31,7 @@ WIDE = 512
 
 FLOPS = 2 * BATCH * SEQ * DIM * FEATURES
 
-SQUARES_AHEAD = 5
+SQUARES_AHEAD = 4
 INVERT_AHEAD = 3
 SCALE_AHEAD = 1
 REGROUP_BEHIND = 1
@@ -184,7 +184,9 @@ def tile_transformerblock_pa_t_kernel(
             result = result_of[first]
             b, t = divmod(first, TILES_PER_BATCH)
             qk, v = product_of[i]
-            for copy, bank, lo, hi in ((nc.scalar.copy, qk, 0, 2), (nc.vector.tensor_copy, v, 2, 3)):
+            squares_left = i + DRAIN_BEHIND + SQUARES_AHEAD < TILES
+            copy_v = nc.vector.tensor_copy if squares_left else nc.scalar.copy
+            for copy, bank, lo, hi in ((nc.scalar.copy, qk, 0, 2), (copy_v, v, 2, 3)):
                 copy(
                     out=result[:, HEADS * lo : HEADS * hi, i - first, :],
                     in_=bank[:].rearrange("p (c j) -> p c j", j=HEAD_DIM),

@@ -185,13 +185,20 @@ def tile_transformerblock_pa_t_kernel(
             b, t = divmod(first, TILES_PER_BATCH)
             qk, v = product_of[i]
             squares_left = i + DRAIN_BEHIND + SQUARES_AHEAD < TILES
-            copy_v = nc.vector.tensor_copy if squares_left else nc.scalar.copy
+            last_pair = first == TILES - PAIR
+            copy_v = nc.vector.tensor_copy if squares_left or last_pair else nc.scalar.copy
             for copy, bank, lo, hi in ((nc.scalar.copy, qk, 0, 2), (copy_v, v, 2, 3)):
                 copy(
                     out=result[:, HEADS * lo : HEADS * hi, i - first, :],
                     in_=bank[:].rearrange("p (c j) -> p c j", j=HEAD_DIM),
                 )
-                if i == first + PAIR - 1:
+                if last_pair:
+                    for which in range(lo, hi):
+                        nc.sync.dma_start(
+                            out=out_rows[which][b, :, :, t + i - first, :],
+                            in_=result[:, HEADS * which : HEADS * (which + 1), i - first, :],
+                        )
+                elif i == first + PAIR - 1:
                     for which in range(lo, hi):
                         nc.sync.dma_start(
                             out=out_rows[which][b, :, :, t : t + PAIR, :],

@@ -101,31 +101,46 @@ def tile_transformerblock_pa_t_kernel(
         )
 
         def square_sum(i):
+            if i == 1:
+                products_of_x = keep.tile([P, DIM], F32)
+                nc.vector.scalar_tensor_tensor(
+                    out=products_of_x[:], in0=x_all[:, i, :], scalar=1.0, in1=x_all[:, i, :],
+                    op0=MULT, op1=MULT, accum_out=sumsq[:, i : i + 1],
+                )
+                return
             squares = ring.tile([P, DIM], BF16)
             nc.scalar.activation(
                 out=squares[:], in_=x_all[:, i, :], func=ACT.Square, accum_out=sumsq[:, i : i + 1]
             )
 
-        def root(i):
+        def served(i):
+            if i < PAIR:
+                return slice(i, i + 1)
             if i % PAIR == PAIR - 1:
-                pair = slice(i + 1 - PAIR, i + 1)
+                return slice(i + 1 - PAIR, i + 1)
+            return None
+
+        def root(i):
+            if served(i) is not None:
                 nc.scalar.activation(
-                    out=rms[:, pair], in_=sumsq[:, pair], func=ACT.Sqrt,
+                    out=rms[:, served(i)], in_=sumsq[:, served(i)], func=ACT.Sqrt,
                     scale=1.0 / DIM, bias=eps[:, 0:1],
                 )
 
         def invert(i):
-            if i % PAIR == PAIR - 1:
-                pair = slice(i + 1 - PAIR, i + 1)
-                nc.vector.reciprocal(out=rstd[:, pair], in_=rms[:, pair])
+            if served(i) is not None:
+                nc.vector.reciprocal(out=rstd[:, served(i)], in_=rms[:, served(i)])
 
         def scale(i):
             y = ring.tile([P, PASSES, PACK, P], F32)
-            nc.gpsimd.tensor_scalar(
-                out=y[:],
-                in0=x_all[:, i, :].rearrange("p (g q j) -> p g j q", g=PASSES, j=PACK),
-                scalar1=rstd[:, i : i + 1], scalar2=1.0, op0=MULT, op1=MULT,
-            )
+            sorted_x = x_all[:, i, :].rearrange("p (g q j) -> p g j q", g=PASSES, j=PACK)
+            if i == 0:
+                nc.vector.tensor_scalar_mul(out=y[:], in0=sorted_x, scalar1=rstd[:, i : i + 1])
+            else:
+                nc.gpsimd.tensor_scalar(
+                    out=y[:], in0=sorted_x,
+                    scalar1=rstd[:, i : i + 1], scalar2=1.0, op0=MULT, op1=MULT,
+                )
             y_of[i] = y
 
         def flip(i):
@@ -211,11 +226,20 @@ def tile_transformerblock_pa_t_kernel(
 
         for step in range(-SQUARES_AHEAD, TILES + DRAIN_BEHIND):
             run(square_sum, step + SQUARES_AHEAD)
-            run(scale, step + SCALE_AHEAD)
+            if step + SCALE_AHEAD > 0:
+                run(scale, step + SCALE_AHEAD)
             run(flip, step)
             run(quantise, step - QUANTISE_BEHIND)
             run(project, step - QUANTISE_BEHIND)
             run(regroup, step - REGROUP_BEHIND)
             run(drain, step - DRAIN_BEHIND)
-            run(invert, step + INVERT_AHEAD)
-            run(root, step + SQUARES_AHEAD)
+            if step + INVERT_AHEAD != 1:
+                run(invert, step + INVERT_AHEAD)
+            if step + INVERT_AHEAD == 2:
+                invert(1)
+            if step + INVERT_AHEAD == 0:
+                scale(0)
+            if step + SQUARES_AHEAD != 1:
+                run(root, step + SQUARES_AHEAD)
+            if step + SQUARES_AHEAD == 2:
+                root(1)

from contextlib import ExitStack

import concourse.mybir as mybir
from concourse.masks import make_identity

BF16 = mybir.dt.bfloat16
F32 = mybir.dt.float32
I32 = mybir.dt.int32
U32 = mybir.dt.uint32
U8 = mybir.dt.uint8
FP8X4 = mybir.dt.float8_e4m3fn_x4
ACT = mybir.ActivationFunctionType
MULT = mybir.AluOpType.mult

P = 128
BATCH = 4
SEQ = 1024
DIM = 1024
HEADS = 2
HEAD_DIM = 128
EPS = 1e-6
FEATURES = 3 * HEADS * HEAD_DIM
BLOCKS = FEATURES // HEAD_DIM
PACK = 4
K_PASS = PACK * P
PASSES = DIM // K_PASS
TILES_PER_BATCH = SEQ // P
TILES = BATCH * TILES_PER_BATCH
PAIR = 2
WIDE = 512

FLOPS = 2 * BATCH * SEQ * DIM * FEATURES

SQUARES_AHEAD = 4
INVERT_AHEAD = 3
SCALE_AHEAD = 1
REGROUP_BEHIND = 1
QUANTISE_BEHIND = 2
DRAIN_BEHIND = 3


def tile_transformerblock_pa_t_kernel(
    tc, x, norm1_w, qkv_w_words, qkv_w_scales, out_0, out_1, out_2
):
    nc = tc.nc
    x_rows = x.rearrange("b (p t) d -> b p t d", t=TILES_PER_BATCH)
    out_rows = [
        o.rearrange("b n (p t) j -> b p n t j", t=TILES_PER_BATCH) for o in (out_0, out_1, out_2)
    ]

    with ExitStack() as ctx:
        ctx.enter_context(tc.manual_schedule())
        keep = ctx.enter_context(tc.tile_pool(name="keep", bufs=1))
        ring = ctx.enter_context(tc.tile_pool(name="ring", bufs=3))
        results = ctx.enter_context(tc.tile_pool(name="results", bufs=4))
        flipped = ctx.enter_context(tc.psum_pool(name="flipped", bufs=2 * PASSES))
        products = ctx.enter_context(tc.psum_pool(name="products", bufs=2))

        x_all = keep.tile([P, TILES, DIM], BF16)
        gain = keep.tile([P, PASSES, PACK], BF16)
        w_words = keep.tile([P, PASSES, FEATURES], U32, align_bytes=64)
        w_scales = keep.tile([P, PASSES, FEATURES], U8, align_bytes=64)
        identity = keep.tile([P, P], F32)
        eps = keep.tile([P, 1], F32)
        first_root = keep.tile([P, 1], F32)
        sumsq = keep.tile([P, TILES], F32)
        rms = keep.tile([P, TILES], F32)
        rstd = keep.tile([P, TILES], F32)

        def load(i):
            b, t = divmod(i, TILES_PER_BATCH)
            nc.sync.dma_start(out=x_all[:, i, :], in_=x_rows[b, :, t, :])

        nc.vector.memset(eps[:], EPS)
        nc.vector.memset(w_scales[:].bitcast(I32), 0)
        make_identity(nc, identity[:])
        nc.scalar.activation(out=first_root[:], in_=eps[:], func=ACT.Sqrt)

        for i in range(SQUARES_AHEAD):
            load(i)
        with nc.allow_non_contiguous_dma(reason="the gain: 256 runs of four values, once"):
            nc.sync.dma_start(
                out=gain[:], in_=norm1_w.rearrange("(g p j) -> p g j", g=PASSES, j=PACK)
            )
        nc.sync.dma_start(
            out=w_words[:].bitcast(I32),
            in_=qkv_w_words.rearrange("g p n t -> p g (n t)").bitcast(I32),
        )
        for quadrant in range(4):
            nc.sync.dma_start(
                out=w_scales[32 * quadrant : 32 * quadrant + 4, :, :].bitcast(I32),
                in_=qkv_w_scales[:, 4 * quadrant : 4 * quadrant + 4, :]
                .rearrange("g r n -> r g n")
                .bitcast(I32),
            )
        for i in range(SQUARES_AHEAD, TILES):
            load(i)

        y_of, flipped_of, grouped_of, codes_of, planes_of, product_of, result_of = (
            {}, {}, {}, {}, {}, {}, {},
        )

        def square_sum(i):
            if i == 1:
                products_of_x = keep.tile([P, DIM], F32)
                nc.vector.scalar_tensor_tensor(
                    out=products_of_x[:], in0=x_all[:, i, :], scalar=1.0, in1=x_all[:, i, :],
                    op0=MULT, op1=MULT, accum_out=sumsq[:, i : i + 1],
                )
                return
            squares = ring.tile([P, DIM], BF16)
            nc.scalar.activation(
                out=squares[:], in_=x_all[:, i, :], func=ACT.Square, accum_out=sumsq[:, i : i + 1]
            )

        def served(i):
            if i < PAIR:
                return slice(i, i + 1)
            if i % PAIR == PAIR - 1:
                return slice(i + 1 - PAIR, i + 1)
            return None

        def root(i):
            if served(i) is not None:
                nc.scalar.activation(
                    out=rms[:, served(i)], in_=sumsq[:, served(i)], func=ACT.Sqrt,
                    scale=1.0 / DIM, bias=eps[:, 0:1],
                )

        def invert(i):
            if served(i) is not None:
                nc.vector.reciprocal(out=rstd[:, served(i)], in_=rms[:, served(i)])

        def scale(i):
            y = ring.tile([P, PASSES, PACK, P], F32)
            sorted_x = x_all[:, i, :].rearrange("p (g q j) -> p g j q", g=PASSES, j=PACK)
            if i == 0:
                nc.vector.tensor_scalar_mul(out=y[:], in0=sorted_x, scalar1=rstd[:, i : i + 1])
            else:
                nc.gpsimd.tensor_scalar(
                    out=y[:], in0=sorted_x,
                    scalar1=rstd[:, i : i + 1], scalar2=1.0, op0=MULT, op1=MULT,
                )
            y_of[i] = y

        def flip(i):
            banks = []
            for g in range(PASSES):
                bank = flipped.tile([P, PACK, P], F32)
                for j in range(PACK):
                    nc.tensor.transpose(
                        out=bank[:, j, :], in_=y_of[i][:, g, j, :], identity=identity[:]
                    )
                banks.append(bank)
            flipped_of[i] = banks

        def regroup(i):
            grouped = ring.tile([P, PASSES, P, PACK], BF16, align_bytes=64)
            for g in range(PASSES):
                nc.vector.tensor_tensor(
                    out=grouped[:, g, :, :],
                    in0=flipped_of[i][g][:].rearrange("p j r -> p r j"),
                    in1=gain[:, g, :].unsqueeze(1).to_broadcast([P, P, PACK]),
                    op=MULT,
                )
            grouped_of[i] = grouped

        def quantise(i):
            codes = ring.tile([P, PASSES, P], U32, align_bytes=64)
            planes = ring.tile([P, PASSES, P], U8, align_bytes=64)
            nc.vector.quantize_mx(
                out=codes[:].rearrange("p g r -> p (g r)").bitcast(FP8X4),
                scales=planes[:].rearrange("p g r -> p (g r)"),
                in_=grouped_of[i][:].rearrange("p g r j -> p (g r j)"),
            )
            codes_of[i], planes_of[i] = codes, planes

        def project(i):
            qk = products.tile([P, WIDE], F32)
            v = products.tile([P, FEATURES - WIDE], F32)
            for acc, cols in ((qk, slice(0, WIDE)), (v, slice(WIDE, FEATURES))):
                for g in range(PASSES):
                    nc.tensor.matmul_mx(
                        out=acc[:],
                        lhsT=codes_of[i][:, g, :].bitcast(FP8X4),
                        lhsT_scale=planes_of[i][:, g, :],
                        rhs=w_words[:, g, cols].bitcast(FP8X4),
                        rhs_scale=w_scales[:, g, cols],
                        start=(g == 0),
                        stop=(g == PASSES - 1),
                    )
            product_of[i] = (qk, v)

        def drain(i):
            first = i - i % PAIR
            if i == first:
                result = results.tile([P, BLOCKS, PAIR, HEAD_DIM], F32)
                result_of[first] = result
            result = result_of[first]
            b, t = divmod(first, TILES_PER_BATCH)
            qk, v = product_of[i]
            squares_left = i + DRAIN_BEHIND + SQUARES_AHEAD < TILES
            last_pair = first == TILES - PAIR
            copy_v = nc.vector.tensor_copy if squares_left or last_pair else nc.scalar.copy
            for copy, bank, lo, hi in ((nc.scalar.copy, qk, 0, 2), (copy_v, v, 2, 3)):
                copy(
                    out=result[:, HEADS * lo : HEADS * hi, i - first, :],
                    in_=bank[:].rearrange("p (c j) -> p c j", j=HEAD_DIM),
                )
                if last_pair:
                    for which in range(lo, hi):
                        nc.sync.dma_start(
                            out=out_rows[which][b, :, :, t + i - first, :],
                            in_=result[:, HEADS * which : HEADS * (which + 1), i - first, :],
                        )
                elif i == first + PAIR - 1:
                    for which in range(lo, hi):
                        nc.sync.dma_start(
                            out=out_rows[which][b, :, :, t : t + PAIR, :],
                            in_=result[:, HEADS * which : HEADS * (which + 1), :, :],
                        )

        def run(stage, i):
            if 0 <= i < TILES:
                stage(i)

        for step in range(-SQUARES_AHEAD, TILES + DRAIN_BEHIND):
            run(square_sum, step + SQUARES_AHEAD)
            if step + SCALE_AHEAD > 0:
                run(scale, step + SCALE_AHEAD)
            run(flip, step)
            run(quantise, step - QUANTISE_BEHIND)
            run(project, step - QUANTISE_BEHIND)
            run(regroup, step - REGROUP_BEHIND)
            run(drain, step - DRAIN_BEHIND)
            if step + INVERT_AHEAD != 1:
                run(invert, step + INVERT_AHEAD)
            if step + INVERT_AHEAD == 2:
                invert(1)
            if step + INVERT_AHEAD == 0:
                scale(0)
            if step + SQUARES_AHEAD != 1:
                run(root, step + SQUARES_AHEAD)
            if step + SQUARES_AHEAD == 2:
                root(1)
